import numpy as np
import ml_dtypes


BF16 = ml_dtypes.bfloat16


def bf(x):
    return np.asarray(x, np.float32).astype(BF16)


def f64(x):
    return np.asarray(x).astype(np.float64)


E2M1 = np.array([0.0, 0.5, 1.0, 1.5, 2.0, 3.0, 4.0, 6.0, -0.0, -0.5, -1.0, -1.5, -2.0, -3.0, -4.0, -6.0])


def pack_weight(w, fmt):
    k, n = w.shape
    w = f64(bf(w)).reshape(k // 32, 32, n)
    amax = np.abs(w).max(1)
    if fmt == "e4m3":
        byte = np.frexp(amax)[1] - 1 + 127 - 7
    else:
        mant, ex = np.frexp(amax / 6.0)
        byte = np.where(mant > 0.5, ex, ex - 1) + 127
    byte = np.clip(np.where(amax > 0, byte, 1), 1, 254)
    scaled = (w * np.exp2(127.0 - byte)[:, None, :]).reshape(k, n).astype(np.float32)
    by_word = np.ascontiguousarray(scaled.reshape(k // 512, 128, 4, n).transpose(0, 1, 3, 2))
    if fmt == "e4m3":
        words = by_word.astype(ml_dtypes.float8_e4m3fn).view(np.uint8)
    else:
        c = by_word.astype(ml_dtypes.float4_e2m1fn).view(np.uint8) & 0xF
        words = c[..., 0::2] | (c[..., 1::2] << 4)
    return np.ascontiguousarray(words), np.ascontiguousarray(byte.astype(np.uint8).reshape(k // 512, 16, n))


def unpack_weight(words, scales, fmt):
    g, p, n, _ = words.shape
    if fmt == "e4m3":
        vals = np.ascontiguousarray(words).view(ml_dtypes.float8_e4m3fn).astype(np.float64)
    else:
        nib = np.empty((g, p, n, 4), np.uint8)
        nib[..., 0::2] = words & 0xF
        nib[..., 1::2] = words >> 4
        vals = E2M1[nib]
    vals = vals * np.repeat(np.exp2(scales.astype(np.float64) - 127.0), 8, axis=1)[..., None]
    return vals.transpose(0, 1, 3, 2).reshape(g * 512, n)

def pack4(w):
    words, scales = pack_weight(w, "e2m1")
    return words.reshape(words.shape[0], 128, -1), scales


def unpack4(words, scales):
    return unpack_weight(words.reshape(words.shape[0], 128, -1, 2), scales, "e2m1")


def kspread(k):
    return np.exp2(np.repeat(np.random.randint(-6, 7, k // 32), 32).astype(np.float64))


B, S, D, H, DK = 4, 128, 3072, 16, 96
E = H * DK
HALF = DK // 2


def rope(t, cos2, sin2):
    t_even = t[..., 0::2]
    t_odd = t[..., 1::2]
    rot = np.stack([-t_odd, t_even], axis=-1).reshape(t.shape)
    return t * cos2 + rot * sin2


def setup_inputs():
    s = kspread(D)
    ang = np.random.uniform(-np.pi, np.pi, (S, HALF))
    x = np.random.standard_normal((B, S, D)) * s
    x_words, x_scales = pack4(x.reshape(B * S, D).T)
    Wq_words, Wq_scales = pack4(np.random.standard_normal((D, E)) / np.sqrt(D) / s[:, None])
    Wk_words, Wk_scales = pack4(np.random.standard_normal((D, E)) / np.sqrt(D) / s[:, None])
    return {"x_words": x_words,
            "x_scales": x_scales,
            "Wq_words": Wq_words,
            "Wq_scales": Wq_scales,
            "Wk_words": Wk_words,
            "Wk_scales": Wk_scales,
            "cos2": bf(np.repeat(np.cos(ang), 2, axis=-1)),
            "sin2": bf(np.repeat(np.sin(ang), 2, axis=-1))}


def reference(x_words, x_scales, Wq_words, Wq_scales, Wk_words, Wk_scales, cos2, sin2):
    xq = unpack4(x_words, x_scales).T.reshape(B, S, D)
    q = (xq @ unpack4(Wq_words, Wq_scales)).reshape(B, S, H, DK).swapaxes(1, 2)
    k = (xq @ unpack4(Wk_words, Wk_scales)).reshape(B, S, H, DK).swapaxes(1, 2)
    c, sn = f64(cos2), f64(sin2)
    return rope(q, c, sn), rope(k, c, sn)

@@ -1,0 +1,179 @@
+from contextlib import ExitStack
+
+import concourse.mybir as mybir
+
+F32 = mybir.dt.float32
+BF16 = mybir.dt.bfloat16
+U8 = mybir.dt.uint8
+I32 = mybir.dt.int32
+FP4X4 = mybir.dt.float4_e2m1fn_x4
+MULT = mybir.AluOpType.mult
+ADD = mybir.AluOpType.add
+
+P = 128
+G = 6
+MB = 4
+E = 1536
+NT = 512
+DK = 96
+ROUNDS = 2
+WARM = 12
+FLOPS = 2 * 512 * 3072 * 3072
+
+
+def tile_multiheadselfattention_pa_kernel(
+    tc, x_words, x_scales, Wq_words, Wq_scales, Wk_words, Wk_scales, cos2, sin2, out_0, out_1
+):
+    nc = tc.nc
+    outs = (out_0, out_1)
+
+    with ExitStack() as ctx:
+        keep = ctx.enter_context(tc.tile_pool(name="keep", bufs=1))
+        prod = ctx.enter_context(tc.tile_pool(name="prod", bufs=6))
+        psum = ctx.enter_context(tc.psum_pool(name="psum", bufs=8))
+        ctx.enter_context(tc.manual_schedule())
+
+        def load_codes(dst, src):
+            nc.sync.dma_start(out=dst.bitcast(I32), in_=src.bitcast(I32))
+
+        def load_scales(plane, src):
+            for q in (0, 2, 1, 3):
+                nc.sync.dma_start(
+                    out=plane[32 * q : 32 * q + 4, :, :].bitcast(I32),
+                    in_=src[:, 4 * q : 4 * q + 4, :].rearrange("g r n -> r g n").bitcast(I32),
+                )
+
+        xs = keep.tile([P, G, 512], U8, name="xs", align_bytes=64)
+        ws_a = keep.tile([P, 2, 1024], U8, name="ws_a", align_bytes=64)
+        ws_b = keep.tile([P, 4, 1024], U8, name="ws_b", align_bytes=64)
+        ws_2 = keep.tile([P, G, 512], U8, name="ws_2", align_bytes=64)
+        ws_k = keep.tile([P, G, E], U8, name="ws_k", align_bytes=64)
+        xc_0 = keep.tile([P, 1, 1024], U8, name="xc_0", align_bytes=64)
+        xc_r = keep.tile([P, 5, 1024], U8, name="xc_r", align_bytes=64)
+        wc_a = [keep.tile([P, 2048], U8, name="wca_%d" % g, align_bytes=64) for g in range(2)]
+        wc_b = [keep.tile([P, 2, 2048], U8, name="wcb_%d" % i, align_bytes=64) for i in range(2)]
+        wc_2 = keep.tile([P, G, 1024], U8, name="wc_2", align_bytes=64)
+        wc_k = [keep.tile([P, 2 * E], U8, name="wck_%d" % g, align_bytes=64) for g in range(G)]
+
+        if WARM:
+            warm = keep.tile([P, NT], BF16, name="warm")
+            nc.gpsimd.memset(warm[:], 0.0)
+        for plane in (xs, ws_a, ws_b, ws_2, ws_k):
+            nc.vector.memset(plane[:].bitcast(I32), 0)
+
+        load_codes(xc_0[:, 0, :], x_words[0])
+        load_codes(wc_a[0][:], Wq_words[0][:, 0:2048])
+        load_scales(xs, x_scales)
+        load_scales(ws_a, Wq_scales[0:2, :, 0:1024])
+        load_codes(xc_r[:], x_words[1:6].rearrange("g p n -> p g n"))
+        load_codes(wc_a[1][:], Wq_words[1][:, 0:2048])
+        load_scales(ws_b, Wq_scales[2:6, :, 0:1024])
+        for i in range(2):
+            load_codes(wc_b[i][:], Wq_words[2 + 2 * i : 4 + 2 * i, :, 0:2048].rearrange("g p n -> p g n"))
+        load_scales(ws_2, Wq_scales[:, :, 1024:1536])
+        load_codes(wc_2[:], Wq_words[:, :, 2048:3072].rearrange("g p n -> p g n"))
+        load_scales(ws_k, Wk_scales)
+        for g in range(G):
+            load_codes(wc_k[g][:], Wk_words[g])
+
+        if WARM:
+            junk = psum.tile([P, NT], F32, name="acc")
+            for i in range(WARM):
+                nc.tensor.matmul(out=junk[:], lhsT=warm[:, 0:P], rhs=warm[:], start=True, stop=True)
+
+        cs = keep.tile([P, DK], BF16, name="cs")
+        sn = keep.tile([P, DK], BF16, name="sn")
+        nc.gpsimd.dma_start(out=cs[:], in_=cos2)
+        nc.gpsimd.dma_start(out=sn[:], in_=sin2)
+        csv = cs[:].rearrange("p (j r) -> p j r", r=2)
+        snv = sn[:].rearrange("p (j r) -> p j r", r=2)
+        one = keep.tile([P, 2, DK // 2, 2], F32, name="one")
+        nc.scalar.copy(out=one[:, 0, :, 0], in_=csv[:, :, 0])
+        nc.scalar.copy(out=one[:, 0, :, 1], in_=snv[:, :, 1])
+        nc.scalar.mul(out=one[:, 1, :, 0], in_=snv[:, :, 0], mul=-1.0)
+        nc.scalar.copy(out=one[:, 1, :, 1], in_=csv[:, :, 1])
+        table = keep.tile([P, 2, 6, DK], F32, name="table")
+        for t in range(2):
+            nc.scalar.copy(
+                out=table[:, t],
+                in_=one[:, t].rearrange("p j r -> p (j r)").unsqueeze(1).to_broadcast([P, 6, DK]),
+            )
+        tab = table[:].rearrange("p t h d -> p t (h d)")
+
+        o_sb = [[keep.tile([P, E], F32, name="o_%d_%d" % (w, m)) for m in range(MB)] for w in range(2)]
+
+        def x_ops(g, m):
+            codes = xc_0[:, 0, :] if g == 0 else xc_r[:, g - 1, :]
+            return codes[:, 256 * m : 256 * (m + 1)], xs[:, g, 128 * m : 128 * (m + 1)]
+
+        def w_ops(w, g, c0, nc_):
+            if w == 1:
+                return wc_k[g][:, 2 * c0 : 2 * (c0 + nc_)], ws_k[:, g, c0 : c0 + nc_]
+            if c0 >= 1024:
+                return wc_2[:, g, 2 * (c0 - 1024) : 2 * (c0 - 1024 + nc_)], ws_2[:, g, c0 - 1024 : c0 - 1024 + nc_]
+            plane = ws_a[:, g, :] if g < 2 else ws_b[:, g - 2, :]
+            codes = wc_a[g][:] if g < 2 else wc_b[(g - 2) // 2][:, g % 2, :]
+            return codes[:, 2 * c0 : 2 * (c0 + nc_)], plane[:, c0 : c0 + nc_]
+
+        def one_pass(acc, w, m, c0, nc_, g):
+            xc, xsc = x_ops(g, m)
+            wc, wsc = w_ops(w, g, c0, nc_)
+            nc.tensor.matmul_mx(
+                out=acc[:],
+                lhsT=xc.bitcast(FP4X4),
+                lhsT_scale=xsc,
+                rhs=wc.bitcast(FP4X4),
+                rhs_scale=wsc,
+                start=(g == 0),
+                stop=(g == G - 1),
+            )
+
+        def rotate(acc, w, m, c0, nc_, adder):
+            off = c0 % DK
+            pr = prod.tile([P, 2, nc_], F32, name="pr")
+            nc.vector.tensor_tensor(
+                out=pr[:].rearrange("p t (j r) -> p t j r", r=2),
+                in0=acc[:].rearrange("p (j t) -> p t j", t=2).unsqueeze(3).to_broadcast([P, 2, nc_ // 2, 2]),
+                in1=tab[:, :, off : off + nc_].rearrange("p t (j r) -> p t j r", r=2),
+                op=MULT,
+            )
+            adder.tensor_tensor(out=o_sb[w][m][:, c0 : c0 + nc_], in0=pr[:, 0, :], in1=pr[:, 1, :], op=ADD)
+
+        def store(w, m, h0, h1):
+            nc.sync.dma_start(
+                out=outs[w][m, h0:h1].rearrange("h p d -> p h d"),
+                in_=o_sb[w][m][:, DK * h0 : DK * h1].rearrange("p (h d) -> p h d", d=DK),
+            )
+
+        first = [(m, n) for m in range(MB) for n in range(2)]
+        accs = [psum.tile([P, NT], F32, name="acc") for i in first]
+        for g in range(ROUNDS):
+            for acc, (m, n) in zip(accs, first):
+                one_pass(acc, 0, m, NT * n, NT, g)
+        for acc, (m, n) in zip(accs, first):
+            for g in range(ROUNDS, G):
+                one_pass(acc, 0, m, NT * n, NT, g)
+            rotate(acc, 0, m, NT * n, NT, nc.gpsimd)
+            if n == 1:
+                store(0, m, 0, 10)
+
+        for w, n in ((0, 2), (1, 0), (1, 1), (1, 2)):
+            for m in range(MB):
+                if (w, n, m) == (1, 2, MB - 1):
+                    break
+                acc = psum.tile([P, NT], F32, name="acc")
+                for g in range(G):
+                    one_pass(acc, w, m, NT * n, NT, g)
+                rotate(acc, w, m, NT * n, NT, nc.gpsimd)
+                if w == 0:
+                    store(0, m, 10, 16)
+                else:
+                    store(1, m, (0, 5, 10)[n], (5, 10, 16)[n])
+
+        for half, adder, h0, h1 in ((0, nc.gpsimd, 10, 13), (1, nc.vector, 13, 16)):
+            c0 = 1024 + 256 * half
+            acc = psum.tile([P, 256], F32, name="acc")
+            for g in range(G):
+                one_pass(acc, 1, MB - 1, c0, 256, g)
+            rotate(acc, 1, MB - 1, c0, 256, adder)
+            store(1, MB - 1, h0, h1)

@@ -16,8 +16,11 @@ MB = 4
 E = 1536
 NT = 512
 DK = 96
-ROUNDS = 2
+ROUNDS = 3
 WARM = 12
+RFORM = True
+SPLIT = False
+TAILPIECES = 4
 FLOPS = 2 * 512 * 3072 * 3072
 
 
@@ -29,19 +32,25 @@ def tile_multiheadselfattention_pa_kernel(
 
     with ExitStack() as ctx:
         keep = ctx.enter_context(tc.tile_pool(name="keep", bufs=1))
-        prod = ctx.enter_context(tc.tile_pool(name="prod", bufs=6))
-        psum = ctx.enter_context(tc.psum_pool(name="psum", bufs=8))
+        psum = ctx.enter_context(tc.psum_pool(name="psum", bufs=1))
         ctx.enter_context(tc.manual_schedule())
 
         def load_codes(dst, src):
             nc.sync.dma_start(out=dst.bitcast(I32), in_=src.bitcast(I32))
 
         def load_scales(plane, src):
-            for q in (0, 2, 1, 3):
-                nc.sync.dma_start(
-                    out=plane[32 * q : 32 * q + 4, :, :].bitcast(I32),
-                    in_=src[:, 4 * q : 4 * q + 4, :].rearrange("g r n -> r g n").bitcast(I32),
-                )
+            for r in range(4):
+                if RFORM:
+                    nc.sync.dma_start(
+                        out=plane[r : P : 32, :, :].bitcast(I32),
+                        in_=src[:, r : 16 : 4, :].rearrange("g q n -> q g n").bitcast(I32),
+                    )
+                else:
+                    q = (0, 2, 1, 3)[r]
+                    nc.sync.dma_start(
+                        out=plane[32 * q : 32 * q + 4, :, :].bitcast(I32),
+                        in_=src[:, 4 * q : 4 * q + 4, :].rearrange("g r n -> r g n").bitcast(I32),
+                    )
 
         xs = keep.tile([P, G, 512], U8, name="xs", align_bytes=64)
         ws_a = keep.tile([P, 2, 1024], U8, name="ws_a", align_bytes=64)
@@ -50,8 +59,7 @@ def tile_multiheadselfattention_pa_kernel(
         ws_k = keep.tile([P, G, E], U8, name="ws_k", align_bytes=64)
         xc_0 = keep.tile([P, 1, 1024], U8, name="xc_0", align_bytes=64)
         xc_r = keep.tile([P, 5, 1024], U8, name="xc_r", align_bytes=64)
-        wc_a = [keep.tile([P, 2048], U8, name="wca_%d" % g, align_bytes=64) for g in range(2)]
-        wc_b = [keep.tile([P, 2, 2048], U8, name="wcb_%d" % i, align_bytes=64) for i in range(2)]
+        wc_q = [keep.tile([P, 2048], U8, name="wcq_%d" % g, align_bytes=64) for g in range(G)]
         wc_2 = keep.tile([P, G, 1024], U8, name="wc_2", align_bytes=64)
         wc_k = [keep.tile([P, 2 * E], U8, name="wck_%d" % g, align_bytes=64) for g in range(G)]
 
@@ -62,22 +70,29 @@ def tile_multiheadselfattention_pa_kernel(
             nc.vector.memset(plane[:].bitcast(I32), 0)
 
         load_codes(xc_0[:, 0, :], x_words[0])
-        load_codes(wc_a[0][:], Wq_words[0][:, 0:2048])
+        load_codes(wc_q[0][:], Wq_words[0][:, 0:2048])
         load_scales(xs, x_scales)
         load_scales(ws_a, Wq_scales[0:2, :, 0:1024])
         load_codes(xc_r[:], x_words[1:6].rearrange("g p n -> p g n"))
-        load_codes(wc_a[1][:], Wq_words[1][:, 0:2048])
+        load_codes(wc_q[1][:], Wq_words[1][:, 0:2048])
         load_scales(ws_b, Wq_scales[2:6, :, 0:1024])
-        for i in range(2):
-            load_codes(wc_b[i][:], Wq_words[2 + 2 * i : 4 + 2 * i, :, 0:2048].rearrange("g p n -> p g n"))
+        for g in range(2, G):
+            load_codes(wc_q[g][:], Wq_words[g][:, 0:2048])
         load_scales(ws_2, Wq_scales[:, :, 1024:1536])
         load_codes(wc_2[:], Wq_words[:, :, 2048:3072].rearrange("g p n -> p g n"))
         load_scales(ws_k, Wk_scales)
         for g in range(G):
             load_codes(wc_k[g][:], Wk_words[g])
 
+        banks = [0]
+
+        def new_bank(width):
+            b = banks[0] % 8
+            banks[0] += 1
+            return psum.tile([P, width], F32, name="acc%d" % b)
+
         if WARM:
-            junk = psum.tile([P, NT], F32, name="acc")
+            junk = new_bank(NT)
             for i in range(WARM):
                 nc.tensor.matmul(out=junk[:], lhsT=warm[:, 0:P], rhs=warm[:], start=True, stop=True)
 
@@ -112,8 +127,7 @@ def tile_multiheadselfattention_pa_kernel(
             if c0 >= 1024:
                 return wc_2[:, g, 2 * (c0 - 1024) : 2 * (c0 - 1024 + nc_)], ws_2[:, g, c0 - 1024 : c0 - 1024 + nc_]
             plane = ws_a[:, g, :] if g < 2 else ws_b[:, g - 2, :]
-            codes = wc_a[g][:] if g < 2 else wc_b[(g - 2) // 2][:, g % 2, :]
-            return codes[:, 2 * c0 : 2 * (c0 + nc_)], plane[:, c0 : c0 + nc_]
+            return wc_q[g][:, 2 * c0 : 2 * (c0 + nc_)], plane[:, c0 : c0 + nc_]
 
         def one_pass(acc, w, m, c0, nc_, g):
             xc, xsc = x_ops(g, m)
@@ -128,9 +142,12 @@ def tile_multiheadselfattention_pa_kernel(
                 stop=(g == G - 1),
             )
 
+        prods = [0]
+
         def rotate(acc, w, m, c0, nc_, adder):
             off = c0 % DK
-            pr = prod.tile([P, 2, nc_], F32, name="pr")
+            pr = keep.tile([P, 2, nc_], F32, name="pr%d" % (prods[0] % 6))
+            prods[0] += 1
             nc.vector.tensor_tensor(
                 out=pr[:].rearrange("p t (j r) -> p t j r", r=2),
                 in0=acc[:].rearrange("p (j t) -> p t j", t=2).unsqueeze(3).to_broadcast([P, 2, nc_ // 2, 2]),
@@ -140,13 +157,16 @@ def tile_multiheadselfattention_pa_kernel(
             adder.tensor_tensor(out=o_sb[w][m][:, c0 : c0 + nc_], in0=pr[:, 0, :], in1=pr[:, 1, :], op=ADD)
 
         def store(w, m, h0, h1):
-            nc.sync.dma_start(
-                out=outs[w][m, h0:h1].rearrange("h p d -> p h d"),
-                in_=o_sb[w][m][:, DK * h0 : DK * h1].rearrange("p (h d) -> p h d", d=DK),
-            )
+            dst = outs[w][m, h0:h1].rearrange("h p d -> p h d")
+            src = o_sb[w][m][:, DK * h0 : DK * h1].rearrange("p (h d) -> p h d", d=DK)
+            if SPLIT:
+                nc.sync.dma_start(out=dst[:, :, 0:64], in_=src[:, :, 0:64])
+                nc.sync.dma_start(out=dst[:, :, 64:96], in_=src[:, :, 64:96])
+            else:
+                nc.sync.dma_start(out=dst, in_=src)
 
         first = [(m, n) for m in range(MB) for n in range(2)]
-        accs = [psum.tile([P, NT], F32, name="acc") for i in first]
+        accs = [new_bank(NT) for i in first]
         for g in range(ROUNDS):
             for acc, (m, n) in zip(accs, first):
                 one_pass(acc, 0, m, NT * n, NT, g)
@@ -157,23 +177,23 @@ def tile_multiheadselfattention_pa_kernel(
             if n == 1:
                 store(0, m, 0, 10)
 
-        for w, n in ((0, 2), (1, 0), (1, 1), (1, 2)):
-            for m in range(MB):
-                if (w, n, m) == (1, 2, MB - 1):
-                    break
-                acc = psum.tile([P, NT], F32, name="acc")
-                for g in range(G):
-                    one_pass(acc, w, m, NT * n, NT, g)
-                rotate(acc, w, m, NT * n, NT, nc.gpsimd)
-                if w == 0:
-                    store(0, m, 10, 16)
-                else:
-                    store(1, m, (0, 5, 10)[n], (5, 10, 16)[n])
-
-        for half, adder, h0, h1 in ((0, nc.gpsimd, 10, 13), (1, nc.vector, 13, 16)):
-            c0 = 1024 + 256 * half
-            acc = psum.tile([P, 256], F32, name="acc")
+        rest = [(w, n, m) for w, n in ((0, 2), (1, 0), (1, 1), (1, 2)) for m in range(MB)]
+        whole = len(rest) - TAILPIECES // 2
+        for w, n, m in rest[:whole]:
+            acc = new_bank(NT)
             for g in range(G):
-                one_pass(acc, 1, MB - 1, c0, 256, g)
-            rotate(acc, 1, MB - 1, c0, 256, adder)
-            store(1, MB - 1, h0, h1)
+                one_pass(acc, w, m, NT * n, NT, g)
+            rotate(acc, w, m, NT * n, NT, nc.gpsimd)
+            if w == 0:
+                store(0, m, 10, 16)
+            else:
+                store(1, m, (0, 5, 10)[n], (5, 10, 16)[n])
+
+        pieces = [(w, n, m, half) for w, n, m in rest[whole:] for half in range(2)]
+        for i, (w, n, m, half) in enumerate(pieces):
+            c0 = NT * n + 256 * half
+            acc = new_bank(256)
+            for g in range(G):
+                one_pass(acc, w, m, c0, 256, g)
+            rotate(acc, w, m, c0, 256, nc.vector if i == len(pieces) - 1 else nc.gpsimd)
+            store(w, m, (10, 13)[half], (13, 16)[half])

@@ -17,7 +17,7 @@ E = 1536
 NT = 512
 DK = 96
 ROUNDS = 3
-WARM = 12
+WARM = 8
 RFORM = True
 SPLIT = False
 TAILPIECES = 4
@@ -52,7 +52,8 @@ def tile_multiheadselfattention_pa_kernel(
                         in_=src[:, 4 * q : 4 * q + 4, :].rearrange("g r n -> r g n").bitcast(I32),
                     )
 
-        xs = keep.tile([P, G, 512], U8, name="xs", align_bytes=64)
+        xs_a = keep.tile([P, 2, 512], U8, name="xs_a", align_bytes=64)
+        xs_b = keep.tile([P, 4, 512], U8, name="xs_b", align_bytes=64)
         ws_a = keep.tile([P, 2, 1024], U8, name="ws_a", align_bytes=64)
         ws_b = keep.tile([P, 4, 1024], U8, name="ws_b", align_bytes=64)
         ws_2 = keep.tile([P, G, 512], U8, name="ws_2", align_bytes=64)
@@ -66,15 +67,16 @@ def tile_multiheadselfattention_pa_kernel(
         if WARM:
             warm = keep.tile([P, NT], BF16, name="warm")
             nc.gpsimd.memset(warm[:], 0.0)
-        for plane in (xs, ws_a, ws_b, ws_2, ws_k):
+        for plane in (xs_a, ws_a, xs_b, ws_b, ws_2, ws_k):
             nc.vector.memset(plane[:].bitcast(I32), 0)
 
         load_codes(xc_0[:, 0, :], x_words[0])
         load_codes(wc_q[0][:], Wq_words[0][:, 0:2048])
-        load_scales(xs, x_scales)
+        load_scales(xs_a, x_scales[0:2])
         load_scales(ws_a, Wq_scales[0:2, :, 0:1024])
         load_codes(xc_r[:], x_words[1:6].rearrange("g p n -> p g n"))
         load_codes(wc_q[1][:], Wq_words[1][:, 0:2048])
+        load_scales(xs_b, x_scales[2:6])
         load_scales(ws_b, Wq_scales[2:6, :, 0:1024])
         for g in range(2, G):
             load_codes(wc_q[g][:], Wq_words[g][:, 0:2048])
@@ -119,7 +121,8 @@ def tile_multiheadselfattention_pa_kernel(
 
         def x_ops(g, m):
             codes = xc_0[:, 0, :] if g == 0 else xc_r[:, g - 1, :]
-            return codes[:, 256 * m : 256 * (m + 1)], xs[:, g, 128 * m : 128 * (m + 1)]
+            plane = xs_a[:, g, :] if g < 2 else xs_b[:, g - 2, :]
+            return codes[:, 256 * m : 256 * (m + 1)], plane[:, 128 * m : 128 * (m + 1)]
 
         def w_ops(w, g, c0, nc_):
             if w == 1:

@@ -57,17 +57,19 @@ def tile_multiheadselfattention_pa_kernel(
         ws_a = keep.tile([P, 2, 1024], U8, name="ws_a", align_bytes=64)
         ws_b = keep.tile([P, 4, 1024], U8, name="ws_b", align_bytes=64)
         ws_2 = keep.tile([P, G, 512], U8, name="ws_2", align_bytes=64)
-        ws_k = keep.tile([P, G, E], U8, name="ws_k", align_bytes=64)
+        ws_k0 = keep.tile([P, G, 512], U8, name="ws_k0", align_bytes=64)
+        ws_k12 = keep.tile([P, G, 1024], U8, name="ws_k12", align_bytes=64)
         xc_0 = keep.tile([P, 1, 1024], U8, name="xc_0", align_bytes=64)
         xc_r = keep.tile([P, 5, 1024], U8, name="xc_r", align_bytes=64)
         wc_q = [keep.tile([P, 2048], U8, name="wcq_%d" % g, align_bytes=64) for g in range(G)]
         wc_2 = keep.tile([P, G, 1024], U8, name="wc_2", align_bytes=64)
-        wc_k = [keep.tile([P, 2 * E], U8, name="wck_%d" % g, align_bytes=64) for g in range(G)]
+        wc_k0 = keep.tile([P, G, 1024], U8, name="wc_k0", align_bytes=64)
+        wc_k12 = [keep.tile([P, 3, 2048], U8, name="wck12_%d" % i, align_bytes=64) for i in range(2)]
 
         if WARM:
             warm = keep.tile([P, NT], BF16, name="warm")
             nc.gpsimd.memset(warm[:], 0.0)
-        for plane in (xs_a, ws_a, xs_b, ws_b, ws_2, ws_k):
+        for plane in (xs_a, ws_a, xs_b, ws_b, ws_2, ws_k0, ws_k12):
             nc.vector.memset(plane[:].bitcast(I32), 0)
 
         load_codes(xc_0[:, 0, :], x_words[0])
@@ -82,9 +84,11 @@ def tile_multiheadselfattention_pa_kernel(
             load_codes(wc_q[g][:], Wq_words[g][:, 0:2048])
         load_scales(ws_2, Wq_scales[:, :, 1024:1536])
         load_codes(wc_2[:], Wq_words[:, :, 2048:3072].rearrange("g p n -> p g n"))
-        load_scales(ws_k, Wk_scales)
-        for g in range(G):
-            load_codes(wc_k[g][:], Wk_words[g])
+        load_scales(ws_k0, Wk_scales[:, :, 0:512])
+        load_codes(wc_k0[:], Wk_words[:, :, 0:1024].rearrange("g p n -> p g n"))
+        load_scales(ws_k12, Wk_scales[:, :, 512:1536])
+        for i in range(2):
+            load_codes(wc_k12[i][:], Wk_words[3 * i : 3 * i + 3, :, 1024:3072].rearrange("g p n -> p g n"))
 
         banks = [0]
 
@@ -125,8 +129,11 @@ def tile_multiheadselfattention_pa_kernel(
             return codes[:, 256 * m : 256 * (m + 1)], plane[:, 128 * m : 128 * (m + 1)]
 
         def w_ops(w, g, c0, nc_):
+            if w == 1 and c0 < 512:
+                return wc_k0[:, g, 2 * c0 : 2 * (c0 + nc_)], ws_k0[:, g, c0 : c0 + nc_]
             if w == 1:
-                return wc_k[g][:, 2 * c0 : 2 * (c0 + nc_)], ws_k[:, g, c0 : c0 + nc_]
+                c1 = c0 - 512
+                return wc_k12[g // 3][:, g % 3, 2 * c1 : 2 * (c1 + nc_)], ws_k12[:, g, c1 : c1 + nc_]
             if c0 >= 1024:
                 return wc_2[:, g, 2 * (c0 - 1024) : 2 * (c0 - 1024 + nc_)], ws_2[:, g, c0 - 1024 : c0 - 1024 + nc_]
             plane = ws_a[:, g, :] if g < 2 else ws_b[:, g - 2, :]

@@ -17,7 +17,7 @@ E = 1536
 NT = 512
 DK = 96
 ROUNDS = 3
-WARM = 8
+WARM = 10
 RFORM = True
 SPLIT = False
 TAILPIECES = 4
@@ -60,7 +60,8 @@ def tile_multiheadselfattention_pa_kernel(
         ws_k0 = keep.tile([P, G, 512], U8, name="ws_k0", align_bytes=64)
         ws_k12 = keep.tile([P, G, 1024], U8, name="ws_k12", align_bytes=64)
         xc_0 = keep.tile([P, 1, 1024], U8, name="xc_0", align_bytes=64)
-        xc_r = keep.tile([P, 5, 1024], U8, name="xc_r", align_bytes=64)
+        xc_1 = keep.tile([P, 2, 1024], U8, name="xc_1", align_bytes=64)
+        xc_3 = keep.tile([P, 3, 1024], U8, name="xc_3", align_bytes=64)
         wc_q = [keep.tile([P, 2048], U8, name="wcq_%d" % g, align_bytes=64) for g in range(G)]
         wc_2 = keep.tile([P, G, 1024], U8, name="wc_2", align_bytes=64)
         wc_k0 = keep.tile([P, G, 1024], U8, name="wc_k0", align_bytes=64)
@@ -76,11 +77,13 @@ def tile_multiheadselfattention_pa_kernel(
         load_codes(wc_q[0][:], Wq_words[0][:, 0:2048])
         load_scales(xs_a, x_scales[0:2])
         load_scales(ws_a, Wq_scales[0:2, :, 0:1024])
-        load_codes(xc_r[:], x_words[1:6].rearrange("g p n -> p g n"))
+        load_codes(xc_1[:], x_words[1:3].rearrange("g p n -> p g n"))
         load_codes(wc_q[1][:], Wq_words[1][:, 0:2048])
         load_scales(xs_b, x_scales[2:6])
         load_scales(ws_b, Wq_scales[2:6, :, 0:1024])
-        for g in range(2, G):
+        load_codes(wc_q[2][:], Wq_words[2][:, 0:2048])
+        load_codes(xc_3[:], x_words[3:6].rearrange("g p n -> p g n"))
+        for g in range(3, G):
             load_codes(wc_q[g][:], Wq_words[g][:, 0:2048])
         load_scales(ws_2, Wq_scales[:, :, 1024:1536])
         load_codes(wc_2[:], Wq_words[:, :, 2048:3072].rearrange("g p n -> p g n"))
@@ -124,7 +127,7 @@ def tile_multiheadselfattention_pa_kernel(
         o_sb = [[keep.tile([P, E], F32, name="o_%d_%d" % (w, m)) for m in range(MB)] for w in range(2)]
 
         def x_ops(g, m):
-            codes = xc_0[:, 0, :] if g == 0 else xc_r[:, g - 1, :]
+            codes = xc_0[:, 0, :] if g == 0 else (xc_1[:, g - 1, :] if g < 3 else xc_3[:, g - 3, :])
             plane = xs_a[:, g, :] if g < 2 else xs_b[:, g - 2, :]
             return codes[:, 256 * m : 256 * (m + 1)], plane[:, 128 * m : 128 * (m + 1)]
 
@@ -180,11 +183,23 @@ def tile_multiheadselfattention_pa_kernel(
         for g in range(ROUNDS):
             for acc, (m, n) in zip(accs, first):
                 one_pass(acc, 0, m, NT * n, NT, g)
+        def multiply(acc, pr, c0, nc_, p0):
+            off = c0 % DK
+            nc.vector.tensor_tensor(
+                out=pr[:, :, p0 : p0 + nc_].rearrange("p t (j r) -> p t j r", r=2),
+                in0=acc[:].rearrange("p (j t) -> p t j", t=2).unsqueeze(3).to_broadcast([P, 2, nc_ // 2, 2]),
+                in1=tab[:, :, off : off + nc_].rearrange("p t (j r) -> p t j r", r=2),
+                op=MULT,
+            )
+
         for acc, (m, n) in zip(accs, first):
             for g in range(ROUNDS, G):
                 one_pass(acc, 0, m, NT * n, NT, g)
-            rotate(acc, 0, m, NT * n, NT, nc.gpsimd)
+            if n == 0:
+                pair = keep.tile([P, 2, 2 * NT], F32, name="pair%d" % m)
+            multiply(acc, pair, NT * n, NT, NT * n)
             if n == 1:
+                nc.gpsimd.tensor_tensor(out=o_sb[0][m][:, 0 : 2 * NT], in0=pair[:, 0, :], in1=pair[:, 1, :], op=ADD)
                 store(0, m, 0, 10)
 
         rest = [(w, n, m) for w, n in ((0, 2), (1, 0), (1, 1), (1, 2)) for m in range(MB)]
@@ -200,10 +215,20 @@ def tile_multiheadselfattention_pa_kernel(
                 store(1, m, (0, 5, 10)[n], (5, 10, 16)[n])
 
         pieces = [(w, n, m, half) for w, n, m in rest[whole:] for half in range(2)]
+        late = []
         for i, (w, n, m, half) in enumerate(pieces):
             c0 = NT * n + 256 * half
             acc = new_bank(256)
             for g in range(G):
                 one_pass(acc, w, m, c0, 256, g)
-            rotate(acc, w, m, c0, 256, nc.vector if i == len(pieces) - 1 else nc.gpsimd)
+            if i < 2:
+                rotate(acc, w, m, c0, 256, nc.gpsimd)
+                store(w, m, (10, 13)[half], (13, 16)[half])
+            else:
+                pr = keep.tile([P, 2, 256], F32, name="pr%d" % (prods[0] % 6))
+                prods[0] += 1
+                multiply(acc, pr, c0, 256, 0)
+                late.append((pr, w, m, c0, half))
+        for pr, w, m, c0, half in late:
+            nc.vector.tensor_tensor(out=o_sb[w][m][:, c0 : c0 + 256], in0=pr[:, 0, :], in1=pr[:, 1, :], op=ADD)
             store(w, m, (10, 13)[half], (13, 16)[half])

@@ -52,46 +52,51 @@ def tile_multiheadselfattention_pa_kernel(
                         in_=src[:, 4 * q : 4 * q + 4, :].rearrange("g r n -> r g n").bitcast(I32),
                     )
 
-        xs_a = keep.tile([P, 2, 512], U8, name="xs_a", align_bytes=64)
-        xs_b = keep.tile([P, 4, 512], U8, name="xs_b", align_bytes=64)
-        ws_a = keep.tile([P, 2, 1024], U8, name="ws_a", align_bytes=64)
-        ws_b = keep.tile([P, 4, 1024], U8, name="ws_b", align_bytes=64)
-        ws_2 = keep.tile([P, G, 512], U8, name="ws_2", align_bytes=64)
-        ws_k0 = keep.tile([P, G, 512], U8, name="ws_k0", align_bytes=64)
-        ws_k12 = keep.tile([P, G, 1024], U8, name="ws_k12", align_bytes=64)
-        xc_0 = keep.tile([P, 1, 1024], U8, name="xc_0", align_bytes=64)
-        xc_1 = keep.tile([P, 2, 1024], U8, name="xc_1", align_bytes=64)
-        xc_3 = keep.tile([P, 3, 1024], U8, name="xc_3", align_bytes=64)
-        wc_q = [keep.tile([P, 2048], U8, name="wcq_%d" % g, align_bytes=64) for g in range(G)]
-        wc_2 = keep.tile([P, G, 1024], U8, name="wc_2", align_bytes=64)
-        wc_k0 = keep.tile([P, G, 1024], U8, name="wc_k0", align_bytes=64)
-        wc_k12 = [keep.tile([P, 3, 2048], U8, name="wck12_%d" % i, align_bytes=64) for i in range(2)]
+        def shifted(passes, width, name, off):
+            whole = keep.tile([P, passes * width + 256], U8, name=name, align_bytes=256)
+            return whole[:, off : off + passes * width].rearrange("p (g c) -> p g c", g=passes)
+
+        XS, WS, XC, WC = 64, 192, 0, 128
+        xs_a = shifted(2, 512, "xs_a", XS)
+        xs_b = shifted(4, 512, "xs_b", XS)
+        ws_a = shifted(2, 1024, "ws_a", WS)
+        ws_b = shifted(4, 1024, "ws_b", WS)
+        ws_2 = shifted(G, 512, "ws_2", WS)
+        ws_k0 = shifted(G, 512, "ws_k0", WS)
+        ws_k12 = shifted(G, 1024, "ws_k12", WS)
+        xc_0 = shifted(1, 1024, "xc_0", XC)
+        xc_1 = shifted(2, 1024, "xc_1", XC)
+        xc_3 = shifted(3, 1024, "xc_3", XC)
+        wc_q = [shifted(1, 2048, "wcq_%d" % g, WC)[:, 0, :] for g in range(G)]
+        wc_2 = shifted(G, 1024, "wc_2", WC)
+        wc_k0 = shifted(G, 1024, "wc_k0", WC)
+        wc_k12 = [shifted(3, 2048, "wck12_%d" % i, WC) for i in range(2)]
 
         if WARM:
             warm = keep.tile([P, NT], BF16, name="warm")
             nc.gpsimd.memset(warm[:], 0.0)
         for plane in (xs_a, ws_a, xs_b, ws_b, ws_2, ws_k0, ws_k12):
-            nc.vector.memset(plane[:].bitcast(I32), 0)
+            nc.vector.memset(plane.bitcast(I32), 0)
 
         load_codes(xc_0[:, 0, :], x_words[0])
-        load_codes(wc_q[0][:], Wq_words[0][:, 0:2048])
+        load_codes(wc_q[0], Wq_words[0][:, 0:2048])
         load_scales(xs_a, x_scales[0:2])
         load_scales(ws_a, Wq_scales[0:2, :, 0:1024])
-        load_codes(xc_1[:], x_words[1:3].rearrange("g p n -> p g n"))
-        load_codes(wc_q[1][:], Wq_words[1][:, 0:2048])
+        load_codes(xc_1, x_words[1:3].rearrange("g p n -> p g n"))
+        load_codes(wc_q[1], Wq_words[1][:, 0:2048])
         load_scales(xs_b, x_scales[2:6])
         load_scales(ws_b, Wq_scales[2:6, :, 0:1024])
-        load_codes(wc_q[2][:], Wq_words[2][:, 0:2048])
-        load_codes(xc_3[:], x_words[3:6].rearrange("g p n -> p g n"))
+        load_codes(wc_q[2], Wq_words[2][:, 0:2048])
+        load_codes(xc_3, x_words[3:6].rearrange("g p n -> p g n"))
         for g in range(3, G):
-            load_codes(wc_q[g][:], Wq_words[g][:, 0:2048])
+            load_codes(wc_q[g], Wq_words[g][:, 0:2048])
         load_scales(ws_2, Wq_scales[:, :, 1024:1536])
-        load_codes(wc_2[:], Wq_words[:, :, 2048:3072].rearrange("g p n -> p g n"))
+        load_codes(wc_2, Wq_words[:, :, 2048:3072].rearrange("g p n -> p g n"))
         load_scales(ws_k0, Wk_scales[:, :, 0:512])
-        load_codes(wc_k0[:], Wk_words[:, :, 0:1024].rearrange("g p n -> p g n"))
+        load_codes(wc_k0, Wk_words[:, :, 0:1024].rearrange("g p n -> p g n"))
         load_scales(ws_k12, Wk_scales[:, :, 512:1536])
         for i in range(2):
-            load_codes(wc_k12[i][:], Wk_words[3 * i : 3 * i + 3, :, 1024:3072].rearrange("g p n -> p g n"))
+            load_codes(wc_k12[i], Wk_words[3 * i : 3 * i + 3, :, 1024:3072].rearrange("g p n -> p g n"))
 
         banks = [0]
 

@@ -17,7 +17,7 @@ E = 1536
 NT = 512
 DK = 96
 ROUNDS = 3
-WARM = 10
+WARM = 8
 RFORM = True
 SPLIT = False
 TAILPIECES = 4
@@ -57,8 +57,8 @@ def tile_multiheadselfattention_pa_kernel(
             return whole[:, off : off + passes * width].rearrange("p (g c) -> p g c", g=passes)
 
         XS, WS, XC, WC = 64, 192, 0, 128
-        xs_a = shifted(2, 512, "xs_a", XS)
-        xs_b = shifted(4, 512, "xs_b", XS)
+        xs_a = shifted(1, 512, "xs_a", XS)
+        xs_b = shifted(5, 512, "xs_b", XS)
         ws_a = shifted(2, 1024, "ws_a", WS)
         ws_b = shifted(4, 1024, "ws_b", WS)
         ws_2 = shifted(G, 512, "ws_2", WS)
@@ -75,16 +75,20 @@ def tile_multiheadselfattention_pa_kernel(
         if WARM:
             warm = keep.tile([P, NT], BF16, name="warm")
             nc.gpsimd.memset(warm[:], 0.0)
-        for plane in (xs_a, ws_a, xs_b, ws_b, ws_2, ws_k0, ws_k12):
+        for plane in (ws_a, xs_b, ws_b, ws_2, ws_k0, ws_k12):
             nc.vector.memset(plane.bitcast(I32), 0)
 
+        for r in range(4):
+            nc.sync.dma_start(
+                out=xs_a[r : P : 4, 0, :].bitcast(I32),
+                in_=x_scales[0][r : 16 : 4, :].bitcast(I32).unsqueeze(1).to_broadcast([4, 8, 128]),
+            )
         load_codes(xc_0[:, 0, :], x_words[0])
         load_codes(wc_q[0], Wq_words[0][:, 0:2048])
-        load_scales(xs_a, x_scales[0:2])
         load_scales(ws_a, Wq_scales[0:2, :, 0:1024])
         load_codes(xc_1, x_words[1:3].rearrange("g p n -> p g n"))
         load_codes(wc_q[1], Wq_words[1][:, 0:2048])
-        load_scales(xs_b, x_scales[2:6])
+        load_scales(xs_b, x_scales[1:6])
         load_scales(ws_b, Wq_scales[2:6, :, 0:1024])
         load_codes(wc_q[2], Wq_words[2][:, 0:2048])
         load_codes(xc_3, x_words[3:6].rearrange("g p n -> p g n"))
@@ -133,7 +137,7 @@ def tile_multiheadselfattention_pa_kernel(
 
         def x_ops(g, m):
             codes = xc_0[:, 0, :] if g == 0 else (xc_1[:, g - 1, :] if g < 3 else xc_3[:, g - 3, :])
-            plane = xs_a[:, g, :] if g < 2 else xs_b[:, g - 2, :]
+            plane = xs_a[:, 0, :] if g == 0 else xs_b[:, g - 1, :]
             return codes[:, 256 * m : 256 * (m + 1)], plane[:, 128 * m : 128 * (m + 1)]
 
         def w_ops(w, g, c0, nc_):

from contextlib import ExitStack

import concourse.mybir as mybir

F32 = mybir.dt.float32
BF16 = mybir.dt.bfloat16
U8 = mybir.dt.uint8
I32 = mybir.dt.int32
FP4X4 = mybir.dt.float4_e2m1fn_x4
MULT = mybir.AluOpType.mult
ADD = mybir.AluOpType.add

P = 128
G = 6
MB = 4
E = 1536
NT = 512
DK = 96
ROUNDS = 3
WARM = 8
RFORM = True
SPLIT = False
TAILPIECES = 4
FLOPS = 2 * 512 * 3072 * 3072


def tile_multiheadselfattention_pa_kernel(
    tc, x_words, x_scales, Wq_words, Wq_scales, Wk_words, Wk_scales, cos2, sin2, out_0, out_1
):
    nc = tc.nc
    outs = (out_0, out_1)

    with ExitStack() as ctx:
        keep = ctx.enter_context(tc.tile_pool(name="keep", bufs=1))
        psum = ctx.enter_context(tc.psum_pool(name="psum", bufs=1))
        ctx.enter_context(tc.manual_schedule())

        def load_codes(dst, src):
            nc.sync.dma_start(out=dst.bitcast(I32), in_=src.bitcast(I32))

        def load_scales(plane, src):
            for r in range(4):
                if RFORM:
                    nc.sync.dma_start(
                        out=plane[r : P : 32, :, :].bitcast(I32),
                        in_=src[:, r : 16 : 4, :].rearrange("g q n -> q g n").bitcast(I32),
                    )
                else:
                    q = (0, 2, 1, 3)[r]
                    nc.sync.dma_start(
                        out=plane[32 * q : 32 * q + 4, :, :].bitcast(I32),
                        in_=src[:, 4 * q : 4 * q + 4, :].rearrange("g r n -> r g n").bitcast(I32),
                    )

        def shifted(passes, width, name, off):
            whole = keep.tile([P, passes * width + 256], U8, name=name, align_bytes=256)
            return whole[:, off : off + passes * width].rearrange("p (g c) -> p g c", g=passes)

        XS, WS, XC, WC = 64, 192, 0, 128
        xs_a = shifted(1, 512, "xs_a", XS)
        xs_b = shifted(5, 512, "xs_b", XS)
        ws_a = shifted(2, 1024, "ws_a", WS)
        ws_b = shifted(4, 1024, "ws_b", WS)
        ws_2 = shifted(G, 512, "ws_2", WS)
        ws_k0 = shifted(G, 512, "ws_k0", WS)
        ws_k12 = shifted(G, 1024, "ws_k12", WS)
        xc_0 = shifted(1, 1024, "xc_0", XC)
        xc_1 = shifted(2, 1024, "xc_1", XC)
        xc_3 = shifted(3, 1024, "xc_3", XC)
        wc_q = [shifted(1, 2048, "wcq_%d" % g, WC)[:, 0, :] for g in range(G)]
        wc_2 = shifted(G, 1024, "wc_2", WC)
        wc_k0 = shifted(G, 1024, "wc_k0", WC)
        wc_k12 = [shifted(3, 2048, "wck12_%d" % i, WC) for i in range(2)]

        if WARM:
            warm = keep.tile([P, NT], BF16, name="warm")
            nc.gpsimd.memset(warm[:], 0.0)
        for plane in (ws_a, xs_b, ws_b, ws_2, ws_k0, ws_k12):
            nc.vector.memset(plane.bitcast(I32), 0)

        for r in range(4):
            nc.sync.dma_start(
                out=xs_a[r : P : 4, 0, :].bitcast(I32),
                in_=x_scales[0][r : 16 : 4, :].bitcast(I32).unsqueeze(1).to_broadcast([4, 8, 128]),
            )
        load_codes(xc_0[:, 0, :], x_words[0])
        load_codes(wc_q[0], Wq_words[0][:, 0:2048])
        load_scales(ws_a, Wq_scales[0:2, :, 0:1024])
        load_codes(xc_1, x_words[1:3].rearrange("g p n -> p g n"))
        load_codes(wc_q[1], Wq_words[1][:, 0:2048])
        load_scales(xs_b, x_scales[1:6])
        load_scales(ws_b, Wq_scales[2:6, :, 0:1024])
        load_codes(wc_q[2], Wq_words[2][:, 0:2048])
        load_codes(xc_3, x_words[3:6].rearrange("g p n -> p g n"))
        for g in range(3, G):
            load_codes(wc_q[g], Wq_words[g][:, 0:2048])
        load_scales(ws_2, Wq_scales[:, :, 1024:1536])
        load_codes(wc_2, Wq_words[:, :, 2048:3072].rearrange("g p n -> p g n"))
        load_scales(ws_k0, Wk_scales[:, :, 0:512])
        load_codes(wc_k0, Wk_words[:, :, 0:1024].rearrange("g p n -> p g n"))
        load_scales(ws_k12, Wk_scales[:, :, 512:1536])
        for i in range(2):
            load_codes(wc_k12[i], Wk_words[3 * i : 3 * i + 3, :, 1024:3072].rearrange("g p n -> p g n"))

        banks = [0]

        def new_bank(width):
            b = banks[0] % 8
            banks[0] += 1
            return psum.tile([P, width], F32, name="acc%d" % b)

        if WARM:
            junk = new_bank(NT)
            for i in range(WARM):
                nc.tensor.matmul(out=junk[:], lhsT=warm[:, 0:P], rhs=warm[:], start=True, stop=True)

        cs = keep.tile([P, DK], BF16, name="cs")
        sn = keep.tile([P, DK], BF16, name="sn")
        nc.gpsimd.dma_start(out=cs[:], in_=cos2)
        nc.gpsimd.dma_start(out=sn[:], in_=sin2)
        csv = cs[:].rearrange("p (j r) -> p j r", r=2)
        snv = sn[:].rearrange("p (j r) -> p j r", r=2)
        one = keep.tile([P, 2, DK // 2, 2], F32, name="one")
        nc.scalar.copy(out=one[:, 0, :, 0], in_=csv[:, :, 0])
        nc.scalar.copy(out=one[:, 0, :, 1], in_=snv[:, :, 1])
        nc.scalar.mul(out=one[:, 1, :, 0], in_=snv[:, :, 0], mul=-1.0)
        nc.scalar.copy(out=one[:, 1, :, 1], in_=csv[:, :, 1])
        table = keep.tile([P, 2, 6, DK], F32, name="table")
        for t in range(2):
            nc.scalar.copy(
                out=table[:, t],
                in_=one[:, t].rearrange("p j r -> p (j r)").unsqueeze(1).to_broadcast([P, 6, DK]),
            )
        tab = table[:].rearrange("p t h d -> p t (h d)")

        o_sb = [[keep.tile([P, E], F32, name="o_%d_%d" % (w, m)) for m in range(MB)] for w in range(2)]

        def x_ops(g, m):
            codes = xc_0[:, 0, :] if g == 0 else (xc_1[:, g - 1, :] if g < 3 else xc_3[:, g - 3, :])
            plane = xs_a[:, 0, :] if g == 0 else xs_b[:, g - 1, :]
            return codes[:, 256 * m : 256 * (m + 1)], plane[:, 128 * m : 128 * (m + 1)]

        def w_ops(w, g, c0, nc_):
            if w == 1 and c0 < 512:
                return wc_k0[:, g, 2 * c0 : 2 * (c0 + nc_)], ws_k0[:, g, c0 : c0 + nc_]
            if w == 1:
                c1 = c0 - 512
                return wc_k12[g // 3][:, g % 3, 2 * c1 : 2 * (c1 + nc_)], ws_k12[:, g, c1 : c1 + nc_]
            if c0 >= 1024:
                return wc_2[:, g, 2 * (c0 - 1024) : 2 * (c0 - 1024 + nc_)], ws_2[:, g, c0 - 1024 : c0 - 1024 + nc_]
            plane = ws_a[:, g, :] if g < 2 else ws_b[:, g - 2, :]
            return wc_q[g][:, 2 * c0 : 2 * (c0 + nc_)], plane[:, c0 : c0 + nc_]

        def one_pass(acc, w, m, c0, nc_, g):
            xc, xsc = x_ops(g, m)
            wc, wsc = w_ops(w, g, c0, nc_)
            nc.tensor.matmul_mx(
                out=acc[:],
                lhsT=xc.bitcast(FP4X4),
                lhsT_scale=xsc,
                rhs=wc.bitcast(FP4X4),
                rhs_scale=wsc,
                start=(g == 0),
                stop=(g == G - 1),
            )

        prods = [0]

        def rotate(acc, w, m, c0, nc_, adder):
            off = c0 % DK
            pr = keep.tile([P, 2, nc_], F32, name="pr%d" % (prods[0] % 6))
            prods[0] += 1
            nc.vector.tensor_tensor(
                out=pr[:].rearrange("p t (j r) -> p t j r", r=2),
                in0=acc[:].rearrange("p (j t) -> p t j", t=2).unsqueeze(3).to_broadcast([P, 2, nc_ // 2, 2]),
                in1=tab[:, :, off : off + nc_].rearrange("p t (j r) -> p t j r", r=2),
                op=MULT,
            )
            adder.tensor_tensor(out=o_sb[w][m][:, c0 : c0 + nc_], in0=pr[:, 0, :], in1=pr[:, 1, :], op=ADD)

        def store(w, m, h0, h1):
            dst = outs[w][m, h0:h1].rearrange("h p d -> p h d")
            src = o_sb[w][m][:, DK * h0 : DK * h1].rearrange("p (h d) -> p h d", d=DK)
            if SPLIT:
                nc.sync.dma_start(out=dst[:, :, 0:64], in_=src[:, :, 0:64])
                nc.sync.dma_start(out=dst[:, :, 64:96], in_=src[:, :, 64:96])
            else:
                nc.sync.dma_start(out=dst, in_=src)

        first = [(m, n) for m in range(MB) for n in range(2)]
        accs = [new_bank(NT) for i in first]
        for g in range(ROUNDS):
            for acc, (m, n) in zip(accs, first):
                one_pass(acc, 0, m, NT * n, NT, g)
        def multiply(acc, pr, c0, nc_, p0):
            off = c0 % DK
            nc.vector.tensor_tensor(
                out=pr[:, :, p0 : p0 + nc_].rearrange("p t (j r) -> p t j r", r=2),
                in0=acc[:].rearrange("p (j t) -> p t j", t=2).unsqueeze(3).to_broadcast([P, 2, nc_ // 2, 2]),
                in1=tab[:, :, off : off + nc_].rearrange("p t (j r) -> p t j r", r=2),
                op=MULT,
            )

        for acc, (m, n) in zip(accs, first):
            for g in range(ROUNDS, G):
                one_pass(acc, 0, m, NT * n, NT, g)
            if n == 0:
                pair = keep.tile([P, 2, 2 * NT], F32, name="pair%d" % m)
            multiply(acc, pair, NT * n, NT, NT * n)
            if n == 1:
                nc.gpsimd.tensor_tensor(out=o_sb[0][m][:, 0 : 2 * NT], in0=pair[:, 0, :], in1=pair[:, 1, :], op=ADD)
                store(0, m, 0, 10)

        rest = [(w, n, m) for w, n in ((0, 2), (1, 0), (1, 1), (1, 2)) for m in range(MB)]
        whole = len(rest) - TAILPIECES // 2
        for w, n, m in rest[:whole]:
            acc = new_bank(NT)
            for g in range(G):
                one_pass(acc, w, m, NT * n, NT, g)
            rotate(acc, w, m, NT * n, NT, nc.gpsimd)
            if w == 0:
                store(0, m, 10, 16)
            else:
                store(1, m, (0, 5, 10)[n], (5, 10, 16)[n])

        pieces = [(w, n, m, half) for w, n, m in rest[whole:] for half in range(2)]
        late = []
        for i, (w, n, m, half) in enumerate(pieces):
            c0 = NT * n + 256 * half
            acc = new_bank(256)
            for g in range(G):
                one_pass(acc, w, m, c0, 256, g)
            if i < 2:
                rotate(acc, w, m, c0, 256, nc.gpsimd)
                store(w, m, (10, 13)[half], (13, 16)[half])
            else:
                pr = keep.tile([P, 2, 256], F32, name="pr%d" % (prods[0] % 6))
                prods[0] += 1
                multiply(acc, pr, c0, 256, 0)
                late.append((pr, w, m, c0, half))
        for pr, w, m, c0, half in late:
            nc.vector.tensor_tensor(out=o_sb[w][m][:, c0 : c0 + 256], in0=pr[:, 0, :], in1=pr[:, 1, :], op=ADD)
            store(w, m, (10, 13)[half], (13, 16)[half])
